import numpy as np
import ml_dtypes


def mxq(x, axis, fmt="e4m3"):
    dtype, down = {"e4m3": (ml_dtypes.float8_e4m3fn, 7), "e5m2": (ml_dtypes.float8_e5m2, 14)}[fmt]
    v = np.moveaxis(np.asarray(x, np.float32).astype(ml_dtypes.bfloat16).astype(np.float64), axis, -1)
    blocks = v.reshape(v.shape[:-1] + (-1, 32))
    amax = np.abs(blocks).max(-1, keepdims=True)
    byte = np.maximum(np.where(amax > 0, np.frexp(amax)[1] - 1 + 127, 0) - down, 1)
    scale = np.exp2(byte - 127.0)
    codes = (blocks / scale).astype(np.float32).astype(dtype).astype(np.float64)
    return np.moveaxis((codes * scale).reshape(v.shape), -1, axis)


WIDE = False


def mx_kscale(k):
    if not WIDE:
        return np.ones(k)
    levels = np.array([20, -20, 10, -10, 0])
    a = np.random.permutation(np.resize(levels, k // 512 * 4)).reshape(k // 512, 4)
    idx = np.arange(k)
    return np.exp2(a[idx // 512, idx % 128 // 32])


BF16 = ml_dtypes.bfloat16


def bf(x):
    return np.asarray(x, np.float32).astype(BF16)


def f64(x):
    return np.asarray(x).astype(np.float64)


B, G, C0, C1, C2, NO = 4, 32, 512, 512, 1024, 512
G0, G1, G2 = G, G // 2, G // 4
N0, N1, N2 = G0 * G0, G1 * G1, G2 * G2
N = N0 + N1 + N2
T = B * N0
STRIDE0, POWER0 = 8.0, 1.0


def sigmoid(v):
    return 1.0 / (1.0 + np.exp(-v))


def setup_inputs():
    s = mx_kscale(T).reshape(B, G0, G0)
    x00 = bf(np.random.standard_normal((B, C0, G0, G0)))
    x1 = bf(np.random.standard_normal((B, C1, G1, G1)))
    x2 = bf(np.random.standard_normal((B, C2, G2, G2)))
    W0 = bf(np.random.standard_normal((NO, C0)) / np.sqrt(C0))
    b0 = bf(np.random.standard_normal(NO) * 0.5)
    W1 = bf(np.random.standard_normal((NO, C1)) / np.sqrt(C1))
    b1 = bf(np.random.standard_normal(NO) * 0.5)
    W2 = bf(np.random.standard_normal((NO, C2)) / np.sqrt(C2))
    b2 = bf(np.random.standard_normal(NO) * 0.5)
    gs = np.ones((B, N, 1))
    gs[:, :N0, 0] = s.reshape(B, N0)
    g = bf(np.random.standard_normal((B, N, NO)) * np.exp2(np.random.randint(-12, 1, (B, N, 1))) * 0.25 / gs)
    p0 = f64(x00).transpose(0, 2, 3, 1).reshape(B, N0, C0) @ f64(W0).T + f64(b0)
    return {
        "x0": bf(f64(x00) * s[:, None, :, :]),
        "x1": x1,
        "x2": x2,
        "W0": W0,
        "b0": b0,
        "W1": W1,
        "b1": b1,
        "W2": W2,
        "b2": b2,
        "p0": np.asarray(p0, np.float32),
        "grad_out": g,
    }


def reference(x0, x1, x2, W0, b0, W1, b1, W2, b2, p0, grad_out):
    g = f64(grad_out)[:, :N0, :].reshape(T, NO)
    y = sigmoid(f64(p0)).reshape(T, NO)
    k = STRIDE0 * 8.0 * POWER0
    dy = g.copy()
    dy[:, 0] = k * y[:, 0] * (g[:, 2] - 0.5 * g[:, 0])
    dy[:, 1] = k * y[:, 1] * (g[:, 3] - 0.5 * g[:, 1])
    dy[:, 2] = k * y[:, 2] * (g[:, 2] + 0.5 * g[:, 0])
    dy[:, 3] = k * y[:, 3] * (g[:, 3] + 0.5 * g[:, 1])
    dp = dy * y * (1.0 - y)
    xt = f64(x0).transpose(0, 2, 3, 1).reshape(T, C0)
    return mxq(dp, 0, "e5m2").T @ mxq(xt, 0, "e4m3")

@@ -1,0 +1,198 @@
+from contextlib import ExitStack
+
+import concourse.mybir as mybir
+from concourse.masks import make_identity
+
+F32 = mybir.dt.float32
+BF16 = mybir.dt.bfloat16
+U32 = mybir.dt.uint32
+U8 = mybir.dt.uint8
+E4M3_X4 = mybir.dt.float8_e4m3fn_x4
+E5M2_X4 = mybir.dt.float8_e5m2_x4
+ACT = mybir.ActivationFunctionType
+ALU = mybir.AluOpType
+
+P = 128
+PACK = 4
+K_PASS = P * PACK
+IMAGES = 4
+CELLS = 1024
+HALVES = CELLS // K_PASS
+PASSES = IMAGES * HALVES
+NO = 512
+C0 = 512
+M_TILES = NO // P
+K_BLOCKS = 2
+BOX = 4
+BOX_GAIN = 64.0
+
+FLOPS = 2 * IMAGES * CELLS * NO * C0
+BYTES = IMAGES * CELLS * (NO * 4 + NO * 2 + C0 * 2) + NO * C0 * 4
+
+
+def tile_objectboxdetect_v_kernel(
+    tc, x0, x1, x2, W0, b0, W1, b1, W2, b2, p0, grad_out, out
+):
+    nc = tc.nc
+    with ExitStack() as ctx:
+        ctx.enter_context(tc.manual_schedule())
+        inputs = ctx.enter_context(tc.tile_pool(name="inputs", bufs=1))
+        consts = ctx.enter_context(tc.tile_pool(name="consts", bufs=1))
+        work = ctx.enter_context(tc.tile_pool(name="work", bufs=3))
+        x_work = ctx.enter_context(tc.tile_pool(name="x_work", bufs=2))
+        results = ctx.enter_context(tc.tile_pool(name="results", bufs=M_TILES))
+        acc_pool = ctx.enter_context(tc.psum_pool(name="acc", bufs=1))
+        xt_pool = ctx.enter_context(tc.psum_pool(name="xt", bufs=HALVES * K_BLOCKS))
+
+        p_sb = []
+        g_sb = []
+        x_sb = []
+        for c in range(PASSES):
+            n, h = divmod(c, HALVES)
+            rows = slice(h * K_PASS, (h + 1) * K_PASS)
+            p_tile = inputs.tile([P, PACK, NO], F32, name="p%d" % c)
+            p_rows = p0[n, rows, :].rearrange("(p j) o -> p j o", j=PACK)
+            for j in range(0, PACK, 2):
+                nc.sync.dma_start(out=p_tile[:, j : j + 2, :], in_=p_rows[:, j : j + 2, :])
+            p_sb.append(p_tile)
+            if h == 0:
+                x_tile = inputs.tile([P, K_BLOCKS * 2 * CELLS], BF16, name="x%d" % n)
+                x_rows = x0[n].rearrange("(b q a) r c -> q b (a r c)", b=K_BLOCKS, a=2)
+                for b in range(K_BLOCKS):
+                    nc.sync.dma_start(
+                        out=x_tile[:, b * 2 * CELLS : (b + 1) * 2 * CELLS], in_=x_rows[:, b, :]
+                    )
+                x_sb.append(x_tile)
+            g_tile = inputs.tile([P, PACK, NO], BF16, name="g%d" % c)
+            nc.sync.dma_start(
+                out=g_tile[:], in_=grad_out[n, rows, :].rearrange("(p j) o -> p j o", j=PACK)
+            )
+            g_sb.append(g_tile)
+
+        ident = consts.tile([P, P], F32, name="ident")
+        make_identity(nc, ident[:])
+
+        acc = [acc_pool.tile([P, C0], F32, name="acc%d" % m) for m in range(M_TILES)]
+
+        def transpose_image(n):
+            words = x_sb[n][:].bitcast(F32).rearrange(
+                "q (b a h p u) -> q b a h u p", b=K_BLOCKS, a=2, h=HALVES, u=2
+            )
+            banks = {}
+            for h in range(HALVES):
+                for b in range(K_BLOCKS):
+                    xt = xt_pool.tile([P, 2, 2, P], F32, name="xt")
+                    for a in range(2):
+                        for u in range(2):
+                            nc.tensor.transpose(xt[:, a, u, :], words[:, b, a, h, u, :], ident[:])
+                    banks[(h, b)] = xt
+            return banks
+
+        def group_image(banks):
+            grouped = x_work.tile([P, HALVES * C0 * PACK], BF16, name="xg", align_bytes=64)
+            grouped_words = grouped[:].bitcast(F32).rearrange(
+                "p (h b w) -> p h b w", h=HALVES, b=K_BLOCKS
+            )
+            for h in range(HALVES):
+                for b in range(K_BLOCKS):
+                    nc.vector.tensor_copy(
+                        out=grouped_words[:, h, b, :].rearrange("p (q a u) -> p q a u", a=2, u=2),
+                        in_=banks[(h, b)][:].rearrange("p a u q -> p q a u"),
+                    )
+            return grouped
+
+        def quantise_image(grouped):
+            codes = x_work.tile([P, HALVES * C0], U32, name="xc", align_bytes=64)
+            scales = x_work.tile([P, HALVES * C0], U8, name="xs", align_bytes=64)
+            nc.vector.quantize_mx(out=codes[:].bitcast(E4M3_X4), scales=scales[:], in_=grouped[:])
+            return codes, scales
+
+        def sigmoid_and_square(c):
+            y = p_sb[c]
+            sq = work.tile([P, PACK, NO], F32, name="sq")
+            for j in range(0, PACK, 2):
+                nc.scalar.activation(out=y[:, j : j + 2, :], in_=y[:, j : j + 2, :], func=ACT.Sigmoid)
+            for j in range(0, PACK, 2):
+                nc.scalar.activation(
+                    out=sq[:, j : j + 2, :], in_=y[:, j : j + 2, :], func=ACT.Square, bias=-0.5
+                )
+            return sq
+
+        def neg_dp(c, sq):
+            y = p_sb[c]
+            g = g_sb[c]
+            grouped = work.tile([P, NO * PACK], BF16, name="dpg", align_bytes=64)
+            view = grouped[:].rearrange("p (o j) -> p o j", j=PACK)
+            spread = work.tile([P, PACK, BOX], F32, name="spread")
+            slope = work.tile([P, PACK, BOX], F32, name="slope")
+            nc.vector.scalar_tensor_tensor(
+                out=spread[:, :, 0:2], in0=g[:, :, 0:2], scalar=-0.5, in1=g[:, :, 2:4],
+                op0=ALU.mult, op1=ALU.add,
+            )
+            nc.vector.scalar_tensor_tensor(
+                out=spread[:, :, 2:4], in0=g[:, :, 0:2], scalar=0.5, in1=g[:, :, 2:4],
+                op0=ALU.mult, op1=ALU.add,
+            )
+            nc.vector.scalar_tensor_tensor(
+                out=slope[:], in0=sq[:, :, 0:BOX], scalar=0.25, in1=y[:, :, 0:BOX],
+                op0=ALU.subtract, op1=ALU.mult,
+            )
+            nc.vector.scalar_tensor_tensor(
+                out=view[:, BOX:, :],
+                in0=sq[:].rearrange("p j o -> p o j")[:, BOX:, :],
+                scalar=0.25,
+                in1=g[:].rearrange("p j o -> p o j")[:, BOX:, :],
+                op0=ALU.subtract, op1=ALU.mult,
+            )
+            nc.vector.scalar_tensor_tensor(
+                out=view[:, 0:BOX, :],
+                in0=slope[:].rearrange("p j o -> p o j"),
+                scalar=BOX_GAIN,
+                in1=spread[:].rearrange("p j o -> p o j"),
+                op0=ALU.mult, op1=ALU.mult,
+            )
+            return grouped
+
+        def quantise_and_multiply(c, grouped, x_codes, x_scales):
+            codes = work.tile([P, NO], U32, name="dc", align_bytes=64)
+            scales = work.tile([P, NO], U8, name="ds", align_bytes=64)
+            nc.vector.quantize_mx(out=codes[:].bitcast(E5M2_X4), scales=scales[:], in_=grouped[:])
+            h = c % HALVES
+            k_cols = slice(h * C0, (h + 1) * C0)
+            for m in range(M_TILES):
+                o_cols = slice(m * P, (m + 1) * P)
+                nc.tensor.matmul_mx(
+                    out=acc[m][:],
+                    lhsT=codes[:, o_cols].bitcast(E5M2_X4),
+                    lhsT_scale=scales[:, o_cols],
+                    rhs=x_codes[:, k_cols].bitcast(E4M3_X4),
+                    rhs_scale=x_scales[:, k_cols],
+                    start=(c == 0),
+                    stop=(c == PASSES - 1),
+                )
+
+        banks = transpose_image(0)
+        x_q = {}
+        waiting = None
+        for c in range(PASSES):
+            n, h = divmod(c, HALVES)
+            sq = sigmoid_and_square(c)
+            if h == 0:
+                x_grouped = group_image(banks)
+            elif n + 1 < IMAGES:
+                banks = transpose_image(n + 1)
+            grouped = neg_dp(c, sq)
+            if c > 0:
+                quantise_and_multiply(c - 1, waiting, *x_q[(c - 1) // HALVES])
+            if h == 0:
+                x_q[n] = quantise_image(x_grouped)
+            waiting = grouped
+        quantise_and_multiply(PASSES - 1, waiting, *x_q[IMAGES - 1])
+
+        for m in range(M_TILES):
+            result = results.tile([P, C0], F32, name="result")
+            if m % 2 == 0:
+                nc.scalar.mul(out=result[:], in_=acc[m][:], mul=-1.0)
+            else:
+                nc.vector.tensor_scalar_mul(out=result[:], in0=acc[m][:], scalar1=-1.0)
+            nc.sync.dma_start(out=out[m * P : (m + 1) * P, :], in_=result[:])

@@ -21,13 +21,19 @@ HALVES = CELLS // K_PASS
 PASSES = IMAGES * HALVES
 NO = 512
 C0 = 512
-M_TILES = NO // P
 K_BLOCKS = 2
+IMAGE_BANKS = HALVES * K_BLOCKS
+SCALAR_BANKS = 1
 BOX = 4
 BOX_GAIN = 64.0
 
 FLOPS = 2 * IMAGES * CELLS * NO * C0
 BYTES = IMAGES * CELLS * (NO * 4 + NO * 2 + C0 * 2) + NO * C0 * 4
+
+
+def pieces_of(c):
+    width = P if c == PASSES - 1 else NO
+    return [(lo, lo + width) for lo in range(0, NO, width)]
 
 
 def tile_objectboxdetect_v_kernel(
@@ -40,9 +46,9 @@ def tile_objectboxdetect_v_kernel(
         consts = ctx.enter_context(tc.tile_pool(name="consts", bufs=1))
         work = ctx.enter_context(tc.tile_pool(name="work", bufs=3))
         x_work = ctx.enter_context(tc.tile_pool(name="x_work", bufs=2))
-        results = ctx.enter_context(tc.tile_pool(name="results", bufs=M_TILES))
+        results = ctx.enter_context(tc.tile_pool(name="results", bufs=NO // P))
         acc_pool = ctx.enter_context(tc.psum_pool(name="acc", bufs=1))
-        xt_pool = ctx.enter_context(tc.psum_pool(name="xt", bufs=HALVES * K_BLOCKS))
+        xt_pool = ctx.enter_context(tc.psum_pool(name="xt", bufs=IMAGE_BANKS))
 
         p_sb = []
         g_sb = []
@@ -72,33 +78,32 @@ def tile_objectboxdetect_v_kernel(
         ident = consts.tile([P, P], F32, name="ident")
         make_identity(nc, ident[:])
 
-        acc = [acc_pool.tile([P, C0], F32, name="acc%d" % m) for m in range(M_TILES)]
+        acc = [acc_pool.tile([P, C0], F32, name="acc%d" % m) for m in range(NO // P)]
 
         def transpose_image(n):
             words = x_sb[n][:].bitcast(F32).rearrange(
                 "q (b a h p u) -> q b a h u p", b=K_BLOCKS, a=2, h=HALVES, u=2
             )
-            banks = {}
+            banks = []
             for h in range(HALVES):
                 for b in range(K_BLOCKS):
                     xt = xt_pool.tile([P, 2, 2, P], F32, name="xt")
                     for a in range(2):
                         for u in range(2):
                             nc.tensor.transpose(xt[:, a, u, :], words[:, b, a, h, u, :], ident[:])
-                    banks[(h, b)] = xt
+                    banks.append(xt)
             return banks
 
         def group_image(banks):
             grouped = x_work.tile([P, HALVES * C0 * PACK], BF16, name="xg", align_bytes=64)
-            grouped_words = grouped[:].bitcast(F32).rearrange(
-                "p (h b w) -> p h b w", h=HALVES, b=K_BLOCKS
-            )
-            for h in range(HALVES):
-                for b in range(K_BLOCKS):
-                    nc.vector.tensor_copy(
-                        out=grouped_words[:, h, b, :].rearrange("p (q a u) -> p q a u", a=2, u=2),
-                        in_=banks[(h, b)][:].rearrange("p a u q -> p q a u"),
-                    )
+            grouped_words = grouped[:].bitcast(F32).rearrange("p (i w) -> p i w", i=IMAGE_BANKS)
+            for i in range(IMAGE_BANKS):
+                dst = grouped_words[:, i, :].rearrange("p (q a u) -> p q a u", a=2, u=2)
+                src = banks[i][:].rearrange("p a u q -> p q a u")
+                if i < IMAGE_BANKS - SCALAR_BANKS:
+                    nc.vector.tensor_copy(out=dst, in_=src)
+                else:
+                    nc.scalar.copy(out=dst, in_=src)
             return grouped
 
         def quantise_image(grouped):
@@ -110,56 +115,61 @@ def tile_objectboxdetect_v_kernel(
         def sigmoid_and_square(c):
             y = p_sb[c]
             sq = work.tile([P, PACK, NO], F32, name="sq")
-            for j in range(0, PACK, 2):
-                nc.scalar.activation(out=y[:, j : j + 2, :], in_=y[:, j : j + 2, :], func=ACT.Sigmoid)
-            for j in range(0, PACK, 2):
-                nc.scalar.activation(
-                    out=sq[:, j : j + 2, :], in_=y[:, j : j + 2, :], func=ACT.Square, bias=-0.5
-                )
+            token_halves = [(slice(j, j + 2), slice(0, NO)) for j in range(0, PACK, 2)]
+            for toks, cols in token_halves:
+                nc.scalar.activation(out=y[:, toks, cols], in_=y[:, toks, cols], func=ACT.Sigmoid)
+            pieces = pieces_of(c)
+            by_piece = [(slice(0, PACK), slice(lo, hi)) for lo, hi in pieces]
+            for toks, cols in token_halves if len(pieces) == 1 else by_piece:
+                nc.scalar.activation(out=sq[:, toks, cols], in_=y[:, toks, cols], func=ACT.Square, bias=-0.5)
             return sq
 
-        def neg_dp(c, sq):
+        def neg_dp(c, sq, grouped, lo, hi):
             y = p_sb[c]
             g = g_sb[c]
-            grouped = work.tile([P, NO * PACK], BF16, name="dpg", align_bytes=64)
             view = grouped[:].rearrange("p (o j) -> p o j", j=PACK)
-            spread = work.tile([P, PACK, BOX], F32, name="spread")
-            slope = work.tile([P, PACK, BOX], F32, name="slope")
+            if lo == 0:
+                spread = work.tile([P, PACK, BOX], F32, name="spread")
+                slope = work.tile([P, PACK, BOX], F32, name="slope")
+                nc.vector.scalar_tensor_tensor(
+                    out=spread[:, :, 0:2], in0=g[:, :, 0:2], scalar=-0.5, in1=g[:, :, 2:4],
+                    op0=ALU.mult, op1=ALU.add,
+                )
+                nc.vector.scalar_tensor_tensor(
+                    out=spread[:, :, 2:4], in0=g[:, :, 0:2], scalar=0.5, in1=g[:, :, 2:4],
+                    op0=ALU.mult, op1=ALU.add,
+                )
+                nc.vector.scalar_tensor_tensor(
+                    out=slope[:], in0=sq[:, :, 0:BOX], scalar=0.25, in1=y[:, :, 0:BOX],
+                    op0=ALU.subtract, op1=ALU.mult,
+                )
+            first = max(lo, BOX)
             nc.vector.scalar_tensor_tensor(
-                out=spread[:, :, 0:2], in0=g[:, :, 0:2], scalar=-0.5, in1=g[:, :, 2:4],
-                op0=ALU.mult, op1=ALU.add,
-            )
-            nc.vector.scalar_tensor_tensor(
-                out=spread[:, :, 2:4], in0=g[:, :, 0:2], scalar=0.5, in1=g[:, :, 2:4],
-                op0=ALU.mult, op1=ALU.add,
-            )
-            nc.vector.scalar_tensor_tensor(
-                out=slope[:], in0=sq[:, :, 0:BOX], scalar=0.25, in1=y[:, :, 0:BOX],
-                op0=ALU.subtract, op1=ALU.mult,
-            )
-            nc.vector.scalar_tensor_tensor(
-                out=view[:, BOX:, :],
-                in0=sq[:].rearrange("p j o -> p o j")[:, BOX:, :],
+                out=view[:, first:hi, :],
+                in0=sq[:].rearrange("p j o -> p o j")[:, first:hi, :],
                 scalar=0.25,
-                in1=g[:].rearrange("p j o -> p o j")[:, BOX:, :],
+                in1=g[:].rearrange("p j o -> p o j")[:, first:hi, :],
                 op0=ALU.subtract, op1=ALU.mult,
             )
-            nc.vector.scalar_tensor_tensor(
-                out=view[:, 0:BOX, :],
-                in0=slope[:].rearrange("p j o -> p o j"),
-                scalar=BOX_GAIN,
-                in1=spread[:].rearrange("p j o -> p o j"),
-                op0=ALU.mult, op1=ALU.mult,
-            )
-            return grouped
+            if lo == 0:
+                nc.vector.scalar_tensor_tensor(
+                    out=view[:, 0:BOX, :],
+                    in0=slope[:].rearrange("p j o -> p o j"),
+                    scalar=BOX_GAIN,
+                    in1=spread[:].rearrange("p j o -> p o j"),
+                    op0=ALU.mult, op1=ALU.mult,
+                )
 
-        def quantise_and_multiply(c, grouped, x_codes, x_scales):
-            codes = work.tile([P, NO], U32, name="dc", align_bytes=64)
-            scales = work.tile([P, NO], U8, name="ds", align_bytes=64)
-            nc.vector.quantize_mx(out=codes[:].bitcast(E5M2_X4), scales=scales[:], in_=grouped[:])
-            h = c % HALVES
+        def quantise_and_multiply(c, grouped, codes, scales, lo, hi):
+            nc.vector.quantize_mx(
+                out=codes[:, lo:hi].bitcast(E5M2_X4),
+                scales=scales[:, lo:hi],
+                in_=grouped[:, lo * PACK : hi * PACK],
+            )
+            n, h = divmod(c, HALVES)
+            x_codes, x_scales = x_q[n]
             k_cols = slice(h * C0, (h + 1) * C0)
-            for m in range(M_TILES):
+            for m in range(lo // P, hi // P):
                 o_cols = slice(m * P, (m + 1) * P)
                 nc.tensor.matmul_mx(
                     out=acc[m][:],
@@ -181,18 +191,19 @@ def tile_objectboxdetect_v_kernel(
                 x_grouped = group_image(banks)
             elif n + 1 < IMAGES:
                 banks = transpose_image(n + 1)
-            grouped = neg_dp(c, sq)
-            if c > 0:
-                quantise_and_multiply(c - 1, waiting, *x_q[(c - 1) // HALVES])
-            if h == 0:
-                x_q[n] = quantise_image(x_grouped)
-            waiting = grouped
-        quantise_and_multiply(PASSES - 1, waiting, *x_q[IMAGES - 1])
+            grouped = work.tile([P, NO * PACK], BF16, name="dpg", align_bytes=64)
+            codes = work.tile([P, NO], U32, name="dc", align_bytes=64)
+            scales = work.tile([P, NO], U8, name="ds", align_bytes=64)
+            for lo, hi in pieces_of(c):
+                neg_dp(c, sq, grouped, lo, hi)
+                if waiting is not None:
+                    quantise_and_multiply(*waiting)
+                if h == 0 and lo == 0:
+                    x_q[n] = quantise_image(x_grouped)
+                waiting = (c, grouped, codes, scales, lo, hi)
+        quantise_and_multiply(*waiting)
 
-        for m in range(M_TILES):
+        for m in range(NO // P):
             result = results.tile([P, C0], F32, name="result")
-            if m % 2 == 0:
-                nc.scalar.mul(out=result[:], in_=acc[m][:], mul=-1.0)
-            else:
-                nc.vector.tensor_scalar_mul(out=result[:], in0=acc[m][:], scalar1=-1.0)
+            nc.scalar.mul(out=result[:], in_=acc[m][:], mul=-1.0)
             nc.sync.dma_start(out=out[m * P : (m + 1) * P, :], in_=result[:])

@@ -23,6 +23,7 @@ NO = 512
 C0 = 512
 K_BLOCKS = 2
 IMAGE_BANKS = HALVES * K_BLOCKS
+BANK_ORDER = [(b, h) for b in range(K_BLOCKS) for h in range(HALVES)]
 SCALAR_BANKS = 1
 BOX = 4
 BOX_GAIN = 64.0
@@ -85,25 +86,26 @@ def tile_objectboxdetect_v_kernel(
                 "q (b a h p u) -> q b a h u p", b=K_BLOCKS, a=2, h=HALVES, u=2
             )
             banks = []
-            for h in range(HALVES):
-                for b in range(K_BLOCKS):
-                    xt = xt_pool.tile([P, 2, 2, P], F32, name="xt")
-                    for a in range(2):
-                        for u in range(2):
-                            nc.tensor.transpose(xt[:, a, u, :], words[:, b, a, h, u, :], ident[:])
-                    banks.append(xt)
+            for b, h in BANK_ORDER:
+                xt = xt_pool.tile([P, 2, 2, P], F32, name="xt")
+                for a in range(2):
+                    for u in range(2):
+                        nc.tensor.transpose(xt[:, a, u, :], words[:, b, a, h, u, :], ident[:])
+                banks.append(xt)
             return banks
 
         def group_image(banks):
             grouped = x_work.tile([P, HALVES * C0 * PACK], BF16, name="xg", align_bytes=64)
-            grouped_words = grouped[:].bitcast(F32).rearrange("p (i w) -> p i w", i=IMAGE_BANKS)
-            for i in range(IMAGE_BANKS):
-                dst = grouped_words[:, i, :].rearrange("p (q a u) -> p q a u", a=2, u=2)
+            grouped_words = grouped[:].bitcast(F32).rearrange(
+                "p (h b w) -> p h b w", h=HALVES, b=K_BLOCKS
+            )
+            for i, (b, h) in enumerate(BANK_ORDER):
+                dst = grouped_words[:, h, b, :].rearrange("p (q a u) -> p q a u", a=2, u=2)
                 src = banks[i][:].rearrange("p a u q -> p q a u")
-                if i < IMAGE_BANKS - SCALAR_BANKS:
-                    nc.vector.tensor_copy(out=dst, in_=src)
-                else:
+                if i < SCALAR_BANKS:
                     nc.scalar.copy(out=dst, in_=src)
+                else:
+                    nc.vector.tensor_copy(out=dst, in_=src)
             return grouped
 
         def quantise_image(grouped):

@@ -24,7 +24,7 @@ C0 = 512
 K_BLOCKS = 2
 IMAGE_BANKS = HALVES * K_BLOCKS
 BANK_ORDER = [(b, h) for b in range(K_BLOCKS) for h in range(HALVES)]
-SCALAR_BANKS = 1
+SCALAR_BANKS = 2
 BOX = 4
 BOX_GAIN = 64.0
 

@@ -37,6 +37,10 @@ def pieces_of(c):
     return [(lo, lo + width) for lo in range(0, NO, width)]
 
 
+def tokens_at_a_time(c):
+    return 1 if c == PASSES - 1 else 2
+
+
 def tile_objectboxdetect_v_kernel(
     tc, x0, x1, x2, W0, b0, W1, b1, W2, b2, p0, grad_out, out
 ):
@@ -59,8 +63,9 @@ def tile_objectboxdetect_v_kernel(
             rows = slice(h * K_PASS, (h + 1) * K_PASS)
             p_tile = inputs.tile([P, PACK, NO], F32, name="p%d" % c)
             p_rows = p0[n, rows, :].rearrange("(p j) o -> p j o", j=PACK)
-            for j in range(0, PACK, 2):
-                nc.sync.dma_start(out=p_tile[:, j : j + 2, :], in_=p_rows[:, j : j + 2, :])
+            for j in range(0, PACK, tokens_at_a_time(c)):
+                toks = slice(j, j + tokens_at_a_time(c))
+                nc.sync.dma_start(out=p_tile[:, toks, :], in_=p_rows[:, toks, :])
             p_sb.append(p_tile)
             if h == 0:
                 x_tile = inputs.tile([P, K_BLOCKS * 2 * CELLS], BF16, name="x%d" % n)
@@ -118,8 +123,9 @@ def tile_objectboxdetect_v_kernel(
             y = p_sb[c]
             sq = work.tile([P, PACK, NO], F32, name="sq")
             token_halves = [(slice(j, j + 2), slice(0, NO)) for j in range(0, PACK, 2)]
-            for toks, cols in token_halves:
-                nc.scalar.activation(out=y[:, toks, cols], in_=y[:, toks, cols], func=ACT.Sigmoid)
+            for j in range(0, PACK, tokens_at_a_time(c)):
+                toks = slice(j, j + tokens_at_a_time(c))
+                nc.scalar.activation(out=y[:, toks, :], in_=y[:, toks, :], func=ACT.Sigmoid)
             pieces = pieces_of(c)
             by_piece = [(slice(0, PACK), slice(lo, hi)) for lo, hi in pieces]
             for toks, cols in token_halves if len(pieces) == 1 else by_piece:
@@ -196,6 +202,9 @@ def tile_objectboxdetect_v_kernel(
             grouped = work.tile([P, NO * PACK], BF16, name="dpg", align_bytes=64)
             codes = work.tile([P, NO], U32, name="dc", align_bytes=64)
             scales = work.tile([P, NO], U8, name="ds", align_bytes=64)
+            if c == PASSES - 1:
+                quantise_and_multiply(*waiting)
+                waiting = None
             for lo, hi in pieces_of(c):
                 neg_dp(c, sq, grouped, lo, hi)
                 if waiting is not None:
@@ -207,5 +216,8 @@ def tile_objectboxdetect_v_kernel(
 
         for m in range(NO // P):
             result = results.tile([P, C0], F32, name="result")
-            nc.scalar.mul(out=result[:], in_=acc[m][:], mul=-1.0)
-            nc.sync.dma_start(out=out[m * P : (m + 1) * P, :], in_=result[:])
+            width = C0 // 2 if m == NO // P - 1 else C0
+            for k0 in range(0, C0, width):
+                cols = slice(k0, k0 + width)
+                nc.scalar.mul(out=result[:, cols], in_=acc[m][:, cols], mul=-1.0)
+                nc.sync.dma_start(out=out[m * P : (m + 1) * P, cols], in_=result[:, cols])

@@ -49,7 +49,7 @@ def tile_objectboxdetect_v_kernel(
         ctx.enter_context(tc.manual_schedule())
         inputs = ctx.enter_context(tc.tile_pool(name="inputs", bufs=1))
         consts = ctx.enter_context(tc.tile_pool(name="consts", bufs=1))
-        work = ctx.enter_context(tc.tile_pool(name="work", bufs=3))
+        work = ctx.enter_context(tc.tile_pool(name="work", bufs=4))
         x_work = ctx.enter_context(tc.tile_pool(name="x_work", bufs=2))
         results = ctx.enter_context(tc.tile_pool(name="results", bufs=NO // P))
         acc_pool = ctx.enter_context(tc.psum_pool(name="acc", bufs=1))

@@ -24,12 +24,17 @@ C0 = 512
 K_BLOCKS = 2
 IMAGE_BANKS = HALVES * K_BLOCKS
 BANK_ORDER = [(b, h) for b in range(K_BLOCKS) for h in range(HALVES)]
-SCALAR_BANKS = 2
+
+
 BOX = 4
 BOX_GAIN = 64.0
 
 FLOPS = 2 * IMAGES * CELLS * NO * C0
 BYTES = IMAGES * CELLS * (NO * 4 + NO * 2 + C0 * 2) + NO * C0 * 4
+
+
+def scalar_banks(n):
+    return IMAGE_BANKS if n == IMAGES - 1 else 2
 
 
 def pieces_of(c):
@@ -49,7 +54,8 @@ def tile_objectboxdetect_v_kernel(
         ctx.enter_context(tc.manual_schedule())
         inputs = ctx.enter_context(tc.tile_pool(name="inputs", bufs=1))
         consts = ctx.enter_context(tc.tile_pool(name="consts", bufs=1))
-        work = ctx.enter_context(tc.tile_pool(name="work", bufs=4))
+        work = ctx.enter_context(tc.tile_pool(name="work", bufs=2))
+        dp_work = ctx.enter_context(tc.tile_pool(name="dp_work", bufs=4))
         x_work = ctx.enter_context(tc.tile_pool(name="x_work", bufs=2))
         results = ctx.enter_context(tc.tile_pool(name="results", bufs=NO // P))
         acc_pool = ctx.enter_context(tc.psum_pool(name="acc", bufs=1))
@@ -61,12 +67,15 @@ def tile_objectboxdetect_v_kernel(
         for c in range(PASSES):
             n, h = divmod(c, HALVES)
             rows = slice(h * K_PASS, (h + 1) * K_PASS)
-            p_tile = inputs.tile([P, PACK, NO], F32, name="p%d" % c)
+            if h == 0:
+                p_tile = inputs.tile([P, HALVES, PACK, NO], F32, name="p%d" % n)
+                g_tile = inputs.tile([P, HALVES, PACK, NO], BF16, name="g%d" % n)
+                p_sb.append(p_tile)
+                g_sb.append(g_tile)
             p_rows = p0[n, rows, :].rearrange("(p j) o -> p j o", j=PACK)
             for j in range(0, PACK, tokens_at_a_time(c)):
                 toks = slice(j, j + tokens_at_a_time(c))
-                nc.sync.dma_start(out=p_tile[:, toks, :], in_=p_rows[:, toks, :])
-            p_sb.append(p_tile)
+                nc.sync.dma_start(out=p_sb[n][:, h, toks, :], in_=p_rows[:, toks, :])
             if h == 0:
                 x_tile = inputs.tile([P, K_BLOCKS * 2 * CELLS], BF16, name="x%d" % n)
                 x_rows = x0[n].rearrange("(b q a) r c -> q b (a r c)", b=K_BLOCKS, a=2)
@@ -75,11 +84,9 @@ def tile_objectboxdetect_v_kernel(
                         out=x_tile[:, b * 2 * CELLS : (b + 1) * 2 * CELLS], in_=x_rows[:, b, :]
                     )
                 x_sb.append(x_tile)
-            g_tile = inputs.tile([P, PACK, NO], BF16, name="g%d" % c)
             nc.sync.dma_start(
-                out=g_tile[:], in_=grad_out[n, rows, :].rearrange("(p j) o -> p j o", j=PACK)
+                out=g_sb[n][:, h, :, :], in_=grad_out[n, rows, :].rearrange("(p j) o -> p j o", j=PACK)
             )
-            g_sb.append(g_tile)
 
         ident = consts.tile([P, P], F32, name="ident")
         make_identity(nc, ident[:])
@@ -99,7 +106,7 @@ def tile_objectboxdetect_v_kernel(
                 banks.append(xt)
             return banks
 
-        def group_image(banks):
+        def group_image(n, banks):
             grouped = x_work.tile([P, HALVES * C0 * PACK], BF16, name="xg", align_bytes=64)
             grouped_words = grouped[:].bitcast(F32).rearrange(
                 "p (h b w) -> p h b w", h=HALVES, b=K_BLOCKS
@@ -107,7 +114,7 @@ def tile_objectboxdetect_v_kernel(
             for i, (b, h) in enumerate(BANK_ORDER):
                 dst = grouped_words[:, h, b, :].rearrange("p (q a u) -> p q a u", a=2, u=2)
                 src = banks[i][:].rearrange("p a u q -> p q a u")
-                if i < SCALAR_BANKS:
+                if i < scalar_banks(n):
                     nc.scalar.copy(out=dst, in_=src)
                 else:
                     nc.vector.tensor_copy(out=dst, in_=src)
@@ -119,9 +126,10 @@ def tile_objectboxdetect_v_kernel(
             nc.vector.quantize_mx(out=codes[:].bitcast(E4M3_X4), scales=scales[:], in_=grouped[:])
             return codes, scales
 
-        def sigmoid_and_square(c):
-            y = p_sb[c]
-            sq = work.tile([P, PACK, NO], F32, name="sq")
+        def sigmoid_and_square(c, sq_of_image):
+            n, h = divmod(c, HALVES)
+            y = p_sb[n][:, h, :, :]
+            sq = sq_of_image[:, h, :, :]
             token_halves = [(slice(j, j + 2), slice(0, NO)) for j in range(0, PACK, 2)]
             for j in range(0, PACK, tokens_at_a_time(c)):
                 toks = slice(j, j + tokens_at_a_time(c))
@@ -130,43 +138,52 @@ def tile_objectboxdetect_v_kernel(
             by_piece = [(slice(0, PACK), slice(lo, hi)) for lo, hi in pieces]
             for toks, cols in token_halves if len(pieces) == 1 else by_piece:
                 nc.scalar.activation(out=sq[:, toks, cols], in_=y[:, toks, cols], func=ACT.Square, bias=-0.5)
-            return sq
 
-        def neg_dp(c, sq, grouped, lo, hi):
-            y = p_sb[c]
-            g = g_sb[c]
+        def box_factors(n, halves, sq_of_image):
+            cells = [P, HALVES * PACK, BOX]
+            spread_tile = work.tile(cells, F32, name="spread")
+            slope_tile = work.tile(cells, F32, name="slope")
+            toks = slice(halves.start * PACK, halves.stop * PACK)
+            g = g_sb[n][:].rearrange("p h j o -> p (h j) o")[:, toks, :]
+            y = p_sb[n][:].rearrange("p h j o -> p (h j) o")[:, toks, :]
+            sq = sq_of_image[:].rearrange("p h j o -> p (h j) o")[:, toks, :]
+            spread = spread_tile[:, toks, :]
+            nc.vector.scalar_tensor_tensor(
+                out=spread[:, :, 0:2], in0=g[:, :, 0:2], scalar=-0.5, in1=g[:, :, 2:4],
+                op0=ALU.mult, op1=ALU.add,
+            )
+            nc.vector.scalar_tensor_tensor(
+                out=spread[:, :, 2:4], in0=g[:, :, 0:2], scalar=0.5, in1=g[:, :, 2:4],
+                op0=ALU.mult, op1=ALU.add,
+            )
+            nc.vector.scalar_tensor_tensor(
+                out=slope_tile[:, toks, :], in0=sq[:, :, 0:BOX], scalar=0.25, in1=y[:, :, 0:BOX],
+                op0=ALU.subtract, op1=ALU.mult,
+            )
+            return spread_tile, slope_tile
+
+        def box_neg_dp(h, factors, grouped):
+            spread, slope = factors
+            toks = slice(h * PACK, (h + 1) * PACK)
+            nc.vector.scalar_tensor_tensor(
+                out=grouped[:].rearrange("p (o j) -> p o j", j=PACK)[:, 0:BOX, :],
+                in0=slope[:, toks, :].rearrange("p j o -> p o j"),
+                scalar=BOX_GAIN,
+                in1=spread[:, toks, :].rearrange("p j o -> p o j"),
+                op0=ALU.mult, op1=ALU.mult,
+            )
+
+        def neg_dp(c, sq_of_image, grouped, lo, hi):
+            n, h = divmod(c, HALVES)
             view = grouped[:].rearrange("p (o j) -> p o j", j=PACK)
-            if lo == 0:
-                spread = work.tile([P, PACK, BOX], F32, name="spread")
-                slope = work.tile([P, PACK, BOX], F32, name="slope")
-                nc.vector.scalar_tensor_tensor(
-                    out=spread[:, :, 0:2], in0=g[:, :, 0:2], scalar=-0.5, in1=g[:, :, 2:4],
-                    op0=ALU.mult, op1=ALU.add,
-                )
-                nc.vector.scalar_tensor_tensor(
-                    out=spread[:, :, 2:4], in0=g[:, :, 0:2], scalar=0.5, in1=g[:, :, 2:4],
-                    op0=ALU.mult, op1=ALU.add,
-                )
-                nc.vector.scalar_tensor_tensor(
-                    out=slope[:], in0=sq[:, :, 0:BOX], scalar=0.25, in1=y[:, :, 0:BOX],
-                    op0=ALU.subtract, op1=ALU.mult,
-                )
             first = max(lo, BOX)
             nc.vector.scalar_tensor_tensor(
                 out=view[:, first:hi, :],
-                in0=sq[:].rearrange("p j o -> p o j")[:, first:hi, :],
+                in0=sq_of_image[:, h, :, :].rearrange("p j o -> p o j")[:, first:hi, :],
                 scalar=0.25,
-                in1=g[:].rearrange("p j o -> p o j")[:, first:hi, :],
+                in1=g_sb[n][:, h, :, :].rearrange("p j o -> p o j")[:, first:hi, :],
                 op0=ALU.subtract, op1=ALU.mult,
             )
-            if lo == 0:
-                nc.vector.scalar_tensor_tensor(
-                    out=view[:, 0:BOX, :],
-                    in0=slope[:].rearrange("p j o -> p o j"),
-                    scalar=BOX_GAIN,
-                    in1=spread[:].rearrange("p j o -> p o j"),
-                    op0=ALU.mult, op1=ALU.mult,
-                )
 
         def quantise_and_multiply(c, grouped, codes, scales, lo, hi):
             nc.vector.quantize_mx(
@@ -194,19 +211,30 @@ def tile_objectboxdetect_v_kernel(
         waiting = None
         for c in range(PASSES):
             n, h = divmod(c, HALVES)
-            sq = sigmoid_and_square(c)
+            last_image = n == IMAGES - 1
             if h == 0:
-                x_grouped = group_image(banks)
+                sq = work.tile([P, HALVES, PACK, NO], F32, name="sq")
+                grouped_of = []
+            sigmoid_and_square(c, sq)
+            if h == 0:
+                x_grouped = group_image(n, banks)
             elif n + 1 < IMAGES:
                 banks = transpose_image(n + 1)
-            grouped = work.tile([P, NO * PACK], BF16, name="dpg", align_bytes=64)
-            codes = work.tile([P, NO], U32, name="dc", align_bytes=64)
-            scales = work.tile([P, NO], U8, name="ds", align_bytes=64)
+            grouped = dp_work.tile([P, NO * PACK], BF16, name="dpg", align_bytes=64)
+            codes = dp_work.tile([P, NO], U32, name="dc", align_bytes=64)
+            scales = dp_work.tile([P, NO], U8, name="ds", align_bytes=64)
+            grouped_of.append(grouped)
             if c == PASSES - 1:
                 quantise_and_multiply(*waiting)
                 waiting = None
+            box = slice(h, h + 1) if last_image else slice(0, HALVES) if h == 1 else None
             for lo, hi in pieces_of(c):
+                if lo == 0 and box is not None:
+                    factors = box_factors(n, box, sq)
                 neg_dp(c, sq, grouped, lo, hi)
+                if lo == 0 and box is not None:
+                    for done in range(box.start, box.stop):
+                        box_neg_dp(done, factors, grouped_of[done])
                 if waiting is not None:
                     quantise_and_multiply(*waiting)
                 if h == 0 and lo == 0:

@@ -26,6 +26,7 @@ IMAGE_BANKS = HALVES * K_BLOCKS
 BANK_ORDER = [(b, h) for b in range(K_BLOCKS) for h in range(HALVES)]
 
 
+PAIR = 2
 BOX = 4
 BOX_GAIN = 64.0
 
@@ -34,16 +35,12 @@ BYTES = IMAGES * CELLS * (NO * 4 + NO * 2 + C0 * 2) + NO * C0 * 4
 
 
 def scalar_banks(n):
-    return IMAGE_BANKS if n == IMAGES - 1 else 2
+    return {0: 2, IMAGES - 1: IMAGE_BANKS}.get(n, 1)
 
 
 def pieces_of(c):
     width = P if c == PASSES - 1 else NO
     return [(lo, lo + width) for lo in range(0, NO, width)]
-
-
-def tokens_at_a_time(c):
-    return 1 if c == PASSES - 1 else 2
 
 
 def tile_objectboxdetect_v_kernel(
@@ -54,7 +51,7 @@ def tile_objectboxdetect_v_kernel(
         ctx.enter_context(tc.manual_schedule())
         inputs = ctx.enter_context(tc.tile_pool(name="inputs", bufs=1))
         consts = ctx.enter_context(tc.tile_pool(name="consts", bufs=1))
-        work = ctx.enter_context(tc.tile_pool(name="work", bufs=2))
+        work = ctx.enter_context(tc.tile_pool(name="work", bufs=3))
         dp_work = ctx.enter_context(tc.tile_pool(name="dp_work", bufs=4))
         x_work = ctx.enter_context(tc.tile_pool(name="x_work", bufs=2))
         results = ctx.enter_context(tc.tile_pool(name="results", bufs=NO // P))
@@ -73,8 +70,8 @@ def tile_objectboxdetect_v_kernel(
                 p_sb.append(p_tile)
                 g_sb.append(g_tile)
             p_rows = p0[n, rows, :].rearrange("(p j) o -> p j o", j=PACK)
-            for j in range(0, PACK, tokens_at_a_time(c)):
-                toks = slice(j, j + tokens_at_a_time(c))
+            for j in range(0, PACK, PAIR):
+                toks = slice(j, j + PAIR)
                 nc.sync.dma_start(out=p_sb[n][:, h, toks, :], in_=p_rows[:, toks, :])
             if h == 0:
                 x_tile = inputs.tile([P, K_BLOCKS * 2 * CELLS], BF16, name="x%d" % n)
@@ -126,28 +123,43 @@ def tile_objectboxdetect_v_kernel(
             nc.vector.quantize_mx(out=codes[:].bitcast(E4M3_X4), scales=scales[:], in_=grouped[:])
             return codes, scales
 
-        def sigmoid_and_square(c, sq_of_image):
+        def squares_of(c):
             n, h = divmod(c, HALVES)
-            y = p_sb[n][:, h, :, :]
-            sq = sq_of_image[:, h, :, :]
-            token_halves = [(slice(j, j + 2), slice(0, NO)) for j in range(0, PACK, 2)]
-            for j in range(0, PACK, tokens_at_a_time(c)):
-                toks = slice(j, j + tokens_at_a_time(c))
-                nc.scalar.activation(out=y[:, toks, :], in_=y[:, toks, :], func=ACT.Sigmoid)
-            pieces = pieces_of(c)
-            by_piece = [(slice(0, PACK), slice(lo, hi)) for lo, hi in pieces]
-            for toks, cols in token_halves if len(pieces) == 1 else by_piece:
-                nc.scalar.activation(out=sq[:, toks, cols], in_=y[:, toks, cols], func=ACT.Square, bias=-0.5)
+            return p_sb[n][:, h, :, :].rearrange("p j o -> p (j o)")
 
-        def box_factors(n, halves, sq_of_image):
-            cells = [P, HALVES * PACK, BOX]
-            spread_tile = work.tile(cells, F32, name="spread")
-            slope_tile = work.tile(cells, F32, name="slope")
+        def sigmoid_and_square(c, y_box):
+            n, h = divmod(c, HALVES)
+            p = p_sb[n][:, h, :, :]
+            y = work.tile([P, PACK // PAIR, NO * PAIR], F32, name="y")
+            for a, cuts in ((0, [(0, NO)]), (1, [(0, NO // 2), (NO // 2, NO)])):
+                for lo, hi in cuts:
+                    nc.scalar.activation(
+                        out=y[:, a, PAIR * lo : PAIR * hi].rearrange("p (o e) -> p o e", e=PAIR),
+                        in_=p[:, PAIR * a : PAIR * (a + 1), lo:hi].rearrange("p e o -> p o e"),
+                        func=ACT.Sigmoid,
+                    )
+            nc.scalar.activation(
+                out=y_box[:, h, :, :], in_=p[:, :, 0:BOX].rearrange("p j o -> p o j"), func=ACT.Sigmoid
+            )
+            pairs = y[:].rearrange("p a (o e) -> p o a e", e=PAIR)
+            pieces = pieces_of(c)
+            for lo, hi in pieces if len(pieces) > 1 else [(0, NO // 2), (NO // 2, NO)]:
+                nc.scalar.activation(
+                    out=squares_of(c)[:, PACK * lo : PACK * hi].rearrange(
+                        "p (o a e) -> p o a e", a=PACK // PAIR, e=PAIR
+                    ),
+                    in_=pairs[:, lo:hi, :, :],
+                    func=ACT.Square,
+                    bias=-0.5,
+                )
+
+        def box_factors(n, halves, y_box):
+            spread_tile = work.tile([P, BOX, HALVES * PACK], F32, name="spread")
+            slope_tile = work.tile([P, HALVES, BOX * PACK], F32, name="slope")
             toks = slice(halves.start * PACK, halves.stop * PACK)
             g = g_sb[n][:].rearrange("p h j o -> p (h j) o")[:, toks, :]
-            y = p_sb[n][:].rearrange("p h j o -> p (h j) o")[:, toks, :]
-            sq = sq_of_image[:].rearrange("p h j o -> p (h j) o")[:, toks, :]
-            spread = spread_tile[:, toks, :]
+            spread = spread_tile[:].rearrange("p o t -> p t o")[:, toks, :]
+            sq = p_sb[n][:].rearrange("p h j o -> p h (j o)")
             nc.vector.scalar_tensor_tensor(
                 out=spread[:, :, 0:2], in0=g[:, :, 0:2], scalar=-0.5, in1=g[:, :, 2:4],
                 op0=ALU.mult, op1=ALU.add,
@@ -157,29 +169,29 @@ def tile_objectboxdetect_v_kernel(
                 op0=ALU.mult, op1=ALU.add,
             )
             nc.vector.scalar_tensor_tensor(
-                out=slope_tile[:, toks, :], in0=sq[:, :, 0:BOX], scalar=0.25, in1=y[:, :, 0:BOX],
+                out=slope_tile[:, halves, :], in0=sq[:, halves, 0 : BOX * PACK], scalar=0.25,
+                in1=y_box[:].rearrange("p h o j -> p h (o j)")[:, halves, :],
                 op0=ALU.subtract, op1=ALU.mult,
             )
             return spread_tile, slope_tile
 
         def box_neg_dp(h, factors, grouped):
             spread, slope = factors
-            toks = slice(h * PACK, (h + 1) * PACK)
             nc.vector.scalar_tensor_tensor(
-                out=grouped[:].rearrange("p (o j) -> p o j", j=PACK)[:, 0:BOX, :],
-                in0=slope[:, toks, :].rearrange("p j o -> p o j"),
+                out=grouped[:, 0 : BOX * PACK].rearrange("p (o j) -> p o j", j=PACK),
+                in0=slope[:, h, :].rearrange("p (o j) -> p o j", j=PACK),
                 scalar=BOX_GAIN,
-                in1=spread[:, toks, :].rearrange("p j o -> p o j"),
+                in1=spread[:, :, h * PACK : (h + 1) * PACK],
                 op0=ALU.mult, op1=ALU.mult,
             )
 
-        def neg_dp(c, sq_of_image, grouped, lo, hi):
+        def neg_dp(c, grouped, lo, hi):
             n, h = divmod(c, HALVES)
-            view = grouped[:].rearrange("p (o j) -> p o j", j=PACK)
             first = max(lo, BOX)
+            run = slice(PACK * first, PACK * hi)
             nc.vector.scalar_tensor_tensor(
-                out=view[:, first:hi, :],
-                in0=sq_of_image[:, h, :, :].rearrange("p j o -> p o j")[:, first:hi, :],
+                out=grouped[:, run].rearrange("p (o j) -> p o j", j=PACK),
+                in0=squares_of(c)[:, run].rearrange("p (o j) -> p o j", j=PACK),
                 scalar=0.25,
                 in1=g_sb[n][:, h, :, :].rearrange("p j o -> p o j")[:, first:hi, :],
                 op0=ALU.subtract, op1=ALU.mult,
@@ -213,9 +225,9 @@ def tile_objectboxdetect_v_kernel(
             n, h = divmod(c, HALVES)
             last_image = n == IMAGES - 1
             if h == 0:
-                sq = work.tile([P, HALVES, PACK, NO], F32, name="sq")
+                y_box = work.tile([P, HALVES, BOX, PACK], F32, name="y_box")
                 grouped_of = []
-            sigmoid_and_square(c, sq)
+            sigmoid_and_square(c, y_box)
             if h == 0:
                 x_grouped = group_image(n, banks)
             elif n + 1 < IMAGES:
@@ -230,8 +242,8 @@ def tile_objectboxdetect_v_kernel(
             box = slice(h, h + 1) if last_image else slice(0, HALVES) if h == 1 else None
             for lo, hi in pieces_of(c):
                 if lo == 0 and box is not None:
-                    factors = box_factors(n, box, sq)
-                neg_dp(c, sq, grouped, lo, hi)
+                    factors = box_factors(n, box, y_box)
+                neg_dp(c, grouped, lo, hi)
                 if lo == 0 and box is not None:
                     for done in range(box.start, box.stop):
                         box_neg_dp(done, factors, grouped_of[done])

@@ -51,7 +51,8 @@ def tile_objectboxdetect_v_kernel(
         ctx.enter_context(tc.manual_schedule())
         inputs = ctx.enter_context(tc.tile_pool(name="inputs", bufs=1))
         consts = ctx.enter_context(tc.tile_pool(name="consts", bufs=1))
-        work = ctx.enter_context(tc.tile_pool(name="work", bufs=3))
+        work = ctx.enter_context(tc.tile_pool(name="work", bufs=2))
+        y_work = ctx.enter_context(tc.tile_pool(name="y_work", bufs=2))
         dp_work = ctx.enter_context(tc.tile_pool(name="dp_work", bufs=4))
         x_work = ctx.enter_context(tc.tile_pool(name="x_work", bufs=2))
         results = ctx.enter_context(tc.tile_pool(name="results", bufs=NO // P))
@@ -123,14 +124,10 @@ def tile_objectboxdetect_v_kernel(
             nc.vector.quantize_mx(out=codes[:].bitcast(E4M3_X4), scales=scales[:], in_=grouped[:])
             return codes, scales
 
-        def squares_of(c):
-            n, h = divmod(c, HALVES)
-            return p_sb[n][:, h, :, :].rearrange("p j o -> p (j o)")
-
-        def sigmoid_and_square(c, y_box):
+        def sigmoid_and_square(c, sq, y_box):
             n, h = divmod(c, HALVES)
             p = p_sb[n][:, h, :, :]
-            y = work.tile([P, PACK // PAIR, NO * PAIR], F32, name="y")
+            y = y_work.tile([P, PACK // PAIR, NO * PAIR], F32, name="y")
             for a, cuts in ((0, [(0, NO)]), (1, [(0, NO // 2), (NO // 2, NO)])):
                 for lo, hi in cuts:
                     nc.scalar.activation(
@@ -145,7 +142,7 @@ def tile_objectboxdetect_v_kernel(
             pieces = pieces_of(c)
             for lo, hi in pieces if len(pieces) > 1 else [(0, NO // 2), (NO // 2, NO)]:
                 nc.scalar.activation(
-                    out=squares_of(c)[:, PACK * lo : PACK * hi].rearrange(
+                    out=sq[:, h, PACK * lo : PACK * hi].rearrange(
                         "p (o a e) -> p o a e", a=PACK // PAIR, e=PAIR
                     ),
                     in_=pairs[:, lo:hi, :, :],
@@ -153,13 +150,12 @@ def tile_objectboxdetect_v_kernel(
                     bias=-0.5,
                 )
 
-        def box_factors(n, halves, y_box):
+        def box_factors(n, halves, sq, y_box):
             spread_tile = work.tile([P, BOX, HALVES * PACK], F32, name="spread")
             slope_tile = work.tile([P, HALVES, BOX * PACK], F32, name="slope")
             toks = slice(halves.start * PACK, halves.stop * PACK)
             g = g_sb[n][:].rearrange("p h j o -> p (h j) o")[:, toks, :]
             spread = spread_tile[:].rearrange("p o t -> p t o")[:, toks, :]
-            sq = p_sb[n][:].rearrange("p h j o -> p h (j o)")
             nc.vector.scalar_tensor_tensor(
                 out=spread[:, :, 0:2], in0=g[:, :, 0:2], scalar=-0.5, in1=g[:, :, 2:4],
                 op0=ALU.mult, op1=ALU.add,
@@ -185,13 +181,13 @@ def tile_objectboxdetect_v_kernel(
                 op0=ALU.mult, op1=ALU.mult,
             )
 
-        def neg_dp(c, grouped, lo, hi):
+        def neg_dp(c, sq, grouped, lo, hi):
             n, h = divmod(c, HALVES)
             first = max(lo, BOX)
             run = slice(PACK * first, PACK * hi)
             nc.vector.scalar_tensor_tensor(
                 out=grouped[:, run].rearrange("p (o j) -> p o j", j=PACK),
-                in0=squares_of(c)[:, run].rearrange("p (o j) -> p o j", j=PACK),
+                in0=sq[:, h, run].rearrange("p (o j) -> p o j", j=PACK),
                 scalar=0.25,
                 in1=g_sb[n][:, h, :, :].rearrange("p j o -> p o j")[:, first:hi, :],
                 op0=ALU.subtract, op1=ALU.mult,
@@ -225,9 +221,10 @@ def tile_objectboxdetect_v_kernel(
             n, h = divmod(c, HALVES)
             last_image = n == IMAGES - 1
             if h == 0:
+                sq = work.tile([P, HALVES, NO * PACK], F32, name="sq")
                 y_box = work.tile([P, HALVES, BOX, PACK], F32, name="y_box")
                 grouped_of = []
-            sigmoid_and_square(c, y_box)
+            sigmoid_and_square(c, sq, y_box)
             if h == 0:
                 x_grouped = group_image(n, banks)
             elif n + 1 < IMAGES:
@@ -242,8 +239,8 @@ def tile_objectboxdetect_v_kernel(
             box = slice(h, h + 1) if last_image else slice(0, HALVES) if h == 1 else None
             for lo, hi in pieces_of(c):
                 if lo == 0 and box is not None:
-                    factors = box_factors(n, box, y_box)
-                neg_dp(c, grouped, lo, hi)
+                    factors = box_factors(n, box, sq, y_box)
+                neg_dp(c, sq, grouped, lo, hi)
                 if lo == 0 and box is not None:
                     for done in range(box.start, box.stop):
                         box_neg_dp(done, factors, grouped_of[done])

@@ -28,6 +28,7 @@ BANK_ORDER = [(b, h) for b in range(K_BLOCKS) for h in range(HALVES)]
 
 PAIR = 2
 BOX = 4
+P_AHEAD = 4
 BOX_GAIN = 64.0
 
 FLOPS = 2 * IMAGES * CELLS * NO * C0
@@ -35,7 +36,7 @@ BYTES = IMAGES * CELLS * (NO * 4 + NO * 2 + C0 * 2) + NO * C0 * 4
 
 
 def scalar_banks(n):
-    return {0: 2, IMAGES - 1: IMAGE_BANKS}.get(n, 1)
+    return IMAGE_BANKS if n == IMAGES - 1 else 0
 
 
 def pieces_of(c):
@@ -62,29 +63,43 @@ def tile_objectboxdetect_v_kernel(
         p_sb = []
         g_sb = []
         x_sb = []
-        for c in range(PASSES):
+        for n in range(IMAGES):
+            p_tile = inputs.tile([P, HALVES, PACK, NO], F32, name="p%d" % n)
+            g_tile = inputs.tile([P, HALVES, PACK, NO], BF16, name="g%d" % n)
+            x_tile = inputs.tile([P, K_BLOCKS * 2 * CELLS], BF16, name="x%d" % n)
+            p_sb.append(p_tile)
+            g_sb.append(g_tile)
+            x_sb.append(x_tile)
+
+        def rows_of(tensor, c):
             n, h = divmod(c, HALVES)
-            rows = slice(h * K_PASS, (h + 1) * K_PASS)
-            if h == 0:
-                p_tile = inputs.tile([P, HALVES, PACK, NO], F32, name="p%d" % n)
-                g_tile = inputs.tile([P, HALVES, PACK, NO], BF16, name="g%d" % n)
-                p_sb.append(p_tile)
-                g_sb.append(g_tile)
-            p_rows = p0[n, rows, :].rearrange("(p j) o -> p j o", j=PACK)
+            rows = tensor[n, h * K_PASS : (h + 1) * K_PASS, :]
+            return rows.rearrange("(p j) o -> p j o", j=PACK)
+
+        def load_p(c):
+            n, h = divmod(c, HALVES)
             for j in range(0, PACK, PAIR):
                 toks = slice(j, j + PAIR)
-                nc.sync.dma_start(out=p_sb[n][:, h, toks, :], in_=p_rows[:, toks, :])
-            if h == 0:
-                x_tile = inputs.tile([P, K_BLOCKS * 2 * CELLS], BF16, name="x%d" % n)
-                x_rows = x0[n].rearrange("(b q a) r c -> q b (a r c)", b=K_BLOCKS, a=2)
-                for b in range(K_BLOCKS):
-                    nc.sync.dma_start(
-                        out=x_tile[:, b * 2 * CELLS : (b + 1) * 2 * CELLS], in_=x_rows[:, b, :]
-                    )
-                x_sb.append(x_tile)
-            nc.sync.dma_start(
-                out=g_sb[n][:, h, :, :], in_=grad_out[n, rows, :].rearrange("(p j) o -> p j o", j=PACK)
-            )
+                nc.sync.dma_start(out=p_sb[n][:, h, toks, :], in_=rows_of(p0, c)[:, toks, :])
+
+        def load_grad(c):
+            n, h = divmod(c, HALVES)
+            nc.sync.dma_start(out=g_sb[n][:, h, :, :], in_=rows_of(grad_out, c))
+
+        def load_x(n):
+            x_rows = x0[n].rearrange("(b q a) r c -> q b (a r c)", b=K_BLOCKS, a=2)
+            for b in range(K_BLOCKS):
+                cols = slice(b * 2 * CELLS, (b + 1) * 2 * CELLS)
+                nc.sync.dma_start(out=x_sb[n][:, cols], in_=x_rows[:, b, :])
+
+        for c in range(PASSES):
+            if c != P_AHEAD + 1:
+                load_p(c)
+            if c % HALVES == 0:
+                load_x(c // HALVES)
+            if c == P_AHEAD:
+                load_p(c + 1)
+            load_grad(c)
 
         ident = consts.tile([P, P], F32, name="ident")
         make_identity(nc, ident[:])
@@ -256,5 +271,8 @@ def tile_objectboxdetect_v_kernel(
             width = C0 // 2 if m == NO // P - 1 else C0
             for k0 in range(0, C0, width):
                 cols = slice(k0, k0 + width)
-                nc.scalar.mul(out=result[:, cols], in_=acc[m][:, cols], mul=-1.0)
+                if m == NO // P - 2:
+                    nc.vector.tensor_scalar_mul(result[:, cols], acc[m][:, cols], -1.0)
+                else:
+                    nc.scalar.mul(out=result[:, cols], in_=acc[m][:, cols], mul=-1.0)
                 nc.sync.dma_start(out=out[m * P : (m + 1) * P, cols], in_=result[:, cols])

@@ -125,8 +125,8 @@ def tile_objectboxdetect_v_kernel(
                 "p (h b w) -> p h b w", h=HALVES, b=K_BLOCKS
             )
             for i, (b, h) in enumerate(BANK_ORDER):
-                dst = grouped_words[:, h, b, :].rearrange("p (q a u) -> p q a u", a=2, u=2)
-                src = banks[i][:].rearrange("p a u q -> p q a u")
+                dst = grouped_words[:, h, b, :].rearrange("p (a q u) -> p a q u", a=2, u=2)
+                src = banks[i][:].rearrange("p a u q -> p a q u")
                 if i < scalar_banks(n):
                     nc.scalar.copy(out=dst, in_=src)
                 else:
@@ -271,8 +271,10 @@ def tile_objectboxdetect_v_kernel(
             width = C0 // 2 if m == NO // P - 1 else C0
             for k0 in range(0, C0, width):
                 cols = slice(k0, k0 + width)
+                dst = result[:, cols].rearrange("p (b q a) -> p b q a", q=P, a=2)
+                src = acc[m][:, cols].rearrange("p (b a q) -> p b q a", q=P, a=2)
                 if m == NO // P - 2:
-                    nc.vector.tensor_scalar_mul(result[:, cols], acc[m][:, cols], -1.0)
+                    nc.vector.tensor_scalar_mul(dst, src, -1.0)
                 else:
-                    nc.scalar.mul(out=result[:, cols], in_=acc[m][:, cols], mul=-1.0)
+                    nc.scalar.mul(out=dst, in_=src, mul=-1.0)
                 nc.sync.dma_start(out=out[m * P : (m + 1) * P, cols], in_=result[:, cols])

@@ -21,14 +21,14 @@ HALVES = CELLS // K_PASS
 PASSES = IMAGES * HALVES
 NO = 512
 C0 = 512
-K_BLOCKS = 2
-IMAGE_BANKS = HALVES * K_BLOCKS
-BANK_ORDER = [(b, h) for b in range(K_BLOCKS) for h in range(HALVES)]
+ROWS = C0 // P
+ROW_PAIRS = 2
+IMAGE_BANKS = HALVES * ROW_PAIRS
+BANK_ORDER = [(b, h) for b in range(ROW_PAIRS) for h in range(HALVES)]
 
 
 PAIR = 2
 BOX = 4
-P_AHEAD = 4
 BOX_GAIN = 64.0
 
 FLOPS = 2 * IMAGES * CELLS * NO * C0
@@ -36,7 +36,7 @@ BYTES = IMAGES * CELLS * (NO * 4 + NO * 2 + C0 * 2) + NO * C0 * 4
 
 
 def scalar_banks(n):
-    return IMAGE_BANKS if n == IMAGES - 1 else 0
+    return {0: 0, IMAGES - 1: IMAGE_BANKS}.get(n, 1)
 
 
 def pieces_of(c):
@@ -66,7 +66,7 @@ def tile_objectboxdetect_v_kernel(
         for n in range(IMAGES):
             p_tile = inputs.tile([P, HALVES, PACK, NO], F32, name="p%d" % n)
             g_tile = inputs.tile([P, HALVES, PACK, NO], BF16, name="g%d" % n)
-            x_tile = inputs.tile([P, K_BLOCKS * 2 * CELLS], BF16, name="x%d" % n)
+            x_tile = inputs.tile([P, ROWS * CELLS], BF16, name="x%d" % n)
             p_sb.append(p_tile)
             g_sb.append(g_tile)
             x_sb.append(x_tile)
@@ -87,18 +87,16 @@ def tile_objectboxdetect_v_kernel(
             nc.sync.dma_start(out=g_sb[n][:, h, :, :], in_=rows_of(grad_out, c))
 
         def load_x(n):
-            x_rows = x0[n].rearrange("(b q a) r c -> q b (a r c)", b=K_BLOCKS, a=2)
-            for b in range(K_BLOCKS):
-                cols = slice(b * 2 * CELLS, (b + 1) * 2 * CELLS)
-                nc.sync.dma_start(out=x_sb[n][:, cols], in_=x_rows[:, b, :])
+            x_rows = x0[n].rearrange("(q a) r c -> q (a r c)", a=ROWS)
+            width = ROWS * CELLS // (ROW_PAIRS if n in (0, IMAGES - 1) else 1)
+            for lo in range(0, ROWS * CELLS, width):
+                cols = slice(lo, lo + width)
+                nc.sync.dma_start(out=x_sb[n][:, cols], in_=x_rows[:, cols])
 
         for c in range(PASSES):
-            if c != P_AHEAD + 1:
-                load_p(c)
+            load_p(c)
             if c % HALVES == 0:
                 load_x(c // HALVES)
-            if c == P_AHEAD:
-                load_p(c + 1)
             load_grad(c)
 
         ident = consts.tile([P, P], F32, name="ident")
@@ -108,7 +106,7 @@ def tile_objectboxdetect_v_kernel(
 
         def transpose_image(n):
             words = x_sb[n][:].bitcast(F32).rearrange(
-                "q (b a h p u) -> q b a h u p", b=K_BLOCKS, a=2, h=HALVES, u=2
+                "q (b a h p u) -> q b a h u p", b=ROW_PAIRS, a=2, h=HALVES, u=2
             )
             banks = []
             for b, h in BANK_ORDER:
@@ -119,19 +117,16 @@ def tile_objectboxdetect_v_kernel(
                 banks.append(xt)
             return banks
 
-        def group_image(n, banks):
-            grouped = x_work.tile([P, HALVES * C0 * PACK], BF16, name="xg", align_bytes=64)
+        def copy_banks(banks, grouped, which, copy):
             grouped_words = grouped[:].bitcast(F32).rearrange(
-                "p (h b w) -> p h b w", h=HALVES, b=K_BLOCKS
+                "p (h b w) -> p h b w", h=HALVES, b=ROW_PAIRS
             )
-            for i, (b, h) in enumerate(BANK_ORDER):
-                dst = grouped_words[:, h, b, :].rearrange("p (a q u) -> p a q u", a=2, u=2)
-                src = banks[i][:].rearrange("p a u q -> p a q u")
-                if i < scalar_banks(n):
-                    nc.scalar.copy(out=dst, in_=src)
-                else:
-                    nc.vector.tensor_copy(out=dst, in_=src)
-            return grouped
+            for i in which:
+                b, h = BANK_ORDER[i]
+                copy(
+                    out=grouped_words[:, h, b, :].rearrange("p (a q u) -> p a q u", a=2, u=2),
+                    in_=banks[i][:].rearrange("p a u q -> p a q u"),
+                )
 
         def quantise_image(grouped):
             codes = x_work.tile([P, HALVES * C0], U32, name="xc", align_bytes=64)
@@ -241,7 +236,11 @@ def tile_objectboxdetect_v_kernel(
                 grouped_of = []
             sigmoid_and_square(c, sq, y_box)
             if h == 0:
-                x_grouped = group_image(n, banks)
+                x_grouped = x_work.tile([P, HALVES * C0 * PACK], BF16, name="xg", align_bytes=64)
+                share = scalar_banks(n)
+                copy_banks(banks, x_grouped, range(share), nc.scalar.copy)
+                if n == 0:
+                    copy_banks(banks, x_grouped, range(share, IMAGE_BANKS), nc.vector.tensor_copy)
             elif n + 1 < IMAGES:
                 banks = transpose_image(n + 1)
             grouped = dp_work.tile([P, NO * PACK], BF16, name="dpg", align_bytes=64)
@@ -259,6 +258,8 @@ def tile_objectboxdetect_v_kernel(
                 if lo == 0 and box is not None:
                     for done in range(box.start, box.stop):
                         box_neg_dp(done, factors, grouped_of[done])
+                if h == 0 and n > 0:
+                    copy_banks(banks, x_grouped, range(share, IMAGE_BANKS), nc.vector.tensor_copy)
                 if waiting is not None:
                     quantise_and_multiply(*waiting)
                 if h == 0 and lo == 0:
@@ -268,13 +269,13 @@ def tile_objectboxdetect_v_kernel(
 
         for m in range(NO // P):
             result = results.tile([P, C0], F32, name="result")
+            by_channel = acc[m][:].rearrange("p (r q) -> p q r", r=ROWS)
             width = C0 // 2 if m == NO // P - 1 else C0
             for k0 in range(0, C0, width):
                 cols = slice(k0, k0 + width)
-                dst = result[:, cols].rearrange("p (b q a) -> p b q a", q=P, a=2)
-                src = acc[m][:, cols].rearrange("p (b a q) -> p b q a", q=P, a=2)
-                if m == NO // P - 2:
-                    nc.vector.tensor_scalar_mul(dst, src, -1.0)
-                else:
-                    nc.scalar.mul(out=dst, in_=src, mul=-1.0)
+                nc.scalar.mul(
+                    out=result[:, cols].rearrange("p (q r) -> p q r", r=ROWS),
+                    in_=by_channel[:, k0 // ROWS : (k0 + width) // ROWS, :],
+                    mul=-1.0,
+                )
                 nc.sync.dma_start(out=out[m * P : (m + 1) * P, cols], in_=result[:, cols])

from contextlib import ExitStack

import concourse.mybir as mybir
from concourse.masks import make_identity

F32 = mybir.dt.float32
BF16 = mybir.dt.bfloat16
U32 = mybir.dt.uint32
U8 = mybir.dt.uint8
E4M3_X4 = mybir.dt.float8_e4m3fn_x4
E5M2_X4 = mybir.dt.float8_e5m2_x4
ACT = mybir.ActivationFunctionType
ALU = mybir.AluOpType

P = 128
PACK = 4
K_PASS = P * PACK
IMAGES = 4
CELLS = 1024
HALVES = CELLS // K_PASS
PASSES = IMAGES * HALVES
NO = 512
C0 = 512
ROWS = C0 // P
ROW_PAIRS = 2
IMAGE_BANKS = HALVES * ROW_PAIRS
BANK_ORDER = [(b, h) for b in range(ROW_PAIRS) for h in range(HALVES)]


PAIR = 2
BOX = 4
BOX_GAIN = 64.0

FLOPS = 2 * IMAGES * CELLS * NO * C0
BYTES = IMAGES * CELLS * (NO * 4 + NO * 2 + C0 * 2) + NO * C0 * 4


def scalar_banks(n):
    return {0: 0, IMAGES - 1: IMAGE_BANKS}.get(n, 1)


def pieces_of(c):
    width = P if c == PASSES - 1 else NO
    return [(lo, lo + width) for lo in range(0, NO, width)]


def tile_objectboxdetect_v_kernel(
    tc, x0, x1, x2, W0, b0, W1, b1, W2, b2, p0, grad_out, out
):
    nc = tc.nc
    with ExitStack() as ctx:
        ctx.enter_context(tc.manual_schedule())
        inputs = ctx.enter_context(tc.tile_pool(name="inputs", bufs=1))
        consts = ctx.enter_context(tc.tile_pool(name="consts", bufs=1))
        work = ctx.enter_context(tc.tile_pool(name="work", bufs=2))
        y_work = ctx.enter_context(tc.tile_pool(name="y_work", bufs=2))
        dp_work = ctx.enter_context(tc.tile_pool(name="dp_work", bufs=4))
        x_work = ctx.enter_context(tc.tile_pool(name="x_work", bufs=2))
        results = ctx.enter_context(tc.tile_pool(name="results", bufs=NO // P))
        acc_pool = ctx.enter_context(tc.psum_pool(name="acc", bufs=1))
        xt_pool = ctx.enter_context(tc.psum_pool(name="xt", bufs=IMAGE_BANKS))

        p_sb = []
        g_sb = []
        x_sb = []
        for n in range(IMAGES):
            p_tile = inputs.tile([P, HALVES, PACK, NO], F32, name="p%d" % n)
            g_tile = inputs.tile([P, HALVES, PACK, NO], BF16, name="g%d" % n)
            x_tile = inputs.tile([P, ROWS * CELLS], BF16, name="x%d" % n)
            p_sb.append(p_tile)
            g_sb.append(g_tile)
            x_sb.append(x_tile)

        def rows_of(tensor, c):
            n, h = divmod(c, HALVES)
            rows = tensor[n, h * K_PASS : (h + 1) * K_PASS, :]
            return rows.rearrange("(p j) o -> p j o", j=PACK)

        def load_p(c):
            n, h = divmod(c, HALVES)
            for j in range(0, PACK, PAIR):
                toks = slice(j, j + PAIR)
                nc.sync.dma_start(out=p_sb[n][:, h, toks, :], in_=rows_of(p0, c)[:, toks, :])

        def load_grad(c):
            n, h = divmod(c, HALVES)
            nc.sync.dma_start(out=g_sb[n][:, h, :, :], in_=rows_of(grad_out, c))

        def load_x(n):
            x_rows = x0[n].rearrange("(q a) r c -> q (a r c)", a=ROWS)
            width = ROWS * CELLS // (ROW_PAIRS if n in (0, IMAGES - 1) else 1)
            for lo in range(0, ROWS * CELLS, width):
                cols = slice(lo, lo + width)
                nc.sync.dma_start(out=x_sb[n][:, cols], in_=x_rows[:, cols])

        for c in range(PASSES):
            load_p(c)
            if c % HALVES == 0:
                load_x(c // HALVES)
            load_grad(c)

        ident = consts.tile([P, P], F32, name="ident")
        make_identity(nc, ident[:])

        acc = [acc_pool.tile([P, C0], F32, name="acc%d" % m) for m in range(NO // P)]

        def transpose_image(n):
            words = x_sb[n][:].bitcast(F32).rearrange(
                "q (b a h p u) -> q b a h u p", b=ROW_PAIRS, a=2, h=HALVES, u=2
            )
            banks = []
            for b, h in BANK_ORDER:
                xt = xt_pool.tile([P, 2, 2, P], F32, name="xt")
                for a in range(2):
                    for u in range(2):
                        nc.tensor.transpose(xt[:, a, u, :], words[:, b, a, h, u, :], ident[:])
                banks.append(xt)
            return banks

        def copy_banks(banks, grouped, which, copy):
            grouped_words = grouped[:].bitcast(F32).rearrange(
                "p (h b w) -> p h b w", h=HALVES, b=ROW_PAIRS
            )
            for i in which:
                b, h = BANK_ORDER[i]
                copy(
                    out=grouped_words[:, h, b, :].rearrange("p (a q u) -> p a q u", a=2, u=2),
                    in_=banks[i][:].rearrange("p a u q -> p a q u"),
                )

        def quantise_image(grouped):
            codes = x_work.tile([P, HALVES * C0], U32, name="xc", align_bytes=64)
            scales = x_work.tile([P, HALVES * C0], U8, name="xs", align_bytes=64)
            nc.vector.quantize_mx(out=codes[:].bitcast(E4M3_X4), scales=scales[:], in_=grouped[:])
            return codes, scales

        def sigmoid_and_square(c, sq, y_box):
            n, h = divmod(c, HALVES)
            p = p_sb[n][:, h, :, :]
            y = y_work.tile([P, PACK // PAIR, NO * PAIR], F32, name="y")
            for a, cuts in ((0, [(0, NO)]), (1, [(0, NO // 2), (NO // 2, NO)])):
                for lo, hi in cuts:
                    nc.scalar.activation(
                        out=y[:, a, PAIR * lo : PAIR * hi].rearrange("p (o e) -> p o e", e=PAIR),
                        in_=p[:, PAIR * a : PAIR * (a + 1), lo:hi].rearrange("p e o -> p o e"),
                        func=ACT.Sigmoid,
                    )
            nc.scalar.activation(
                out=y_box[:, h, :, :], in_=p[:, :, 0:BOX].rearrange("p j o -> p o j"), func=ACT.Sigmoid
            )
            pairs = y[:].rearrange("p a (o e) -> p o a e", e=PAIR)
            pieces = pieces_of(c)
            for lo, hi in pieces if len(pieces) > 1 else [(0, NO // 2), (NO // 2, NO)]:
                nc.scalar.activation(
                    out=sq[:, h, PACK * lo : PACK * hi].rearrange(
                        "p (o a e) -> p o a e", a=PACK // PAIR, e=PAIR
                    ),
                    in_=pairs[:, lo:hi, :, :],
                    func=ACT.Square,
                    bias=-0.5,
                )

        def box_factors(n, halves, sq, y_box):
            spread_tile = work.tile([P, BOX, HALVES * PACK], F32, name="spread")
            slope_tile = work.tile([P, HALVES, BOX * PACK], F32, name="slope")
            toks = slice(halves.start * PACK, halves.stop * PACK)
            g = g_sb[n][:].rearrange("p h j o -> p (h j) o")[:, toks, :]
            spread = spread_tile[:].rearrange("p o t -> p t o")[:, toks, :]
            nc.vector.scalar_tensor_tensor(
                out=spread[:, :, 0:2], in0=g[:, :, 0:2], scalar=-0.5, in1=g[:, :, 2:4],
                op0=ALU.mult, op1=ALU.add,
            )
            nc.vector.scalar_tensor_tensor(
                out=spread[:, :, 2:4], in0=g[:, :, 0:2], scalar=0.5, in1=g[:, :, 2:4],
                op0=ALU.mult, op1=ALU.add,
            )
            nc.vector.scalar_tensor_tensor(
                out=slope_tile[:, halves, :], in0=sq[:, halves, 0 : BOX * PACK], scalar=0.25,
                in1=y_box[:].rearrange("p h o j -> p h (o j)")[:, halves, :],
                op0=ALU.subtract, op1=ALU.mult,
            )
            return spread_tile, slope_tile

        def box_neg_dp(h, factors, grouped):
            spread, slope = factors
            nc.vector.scalar_tensor_tensor(
                out=grouped[:, 0 : BOX * PACK].rearrange("p (o j) -> p o j", j=PACK),
                in0=slope[:, h, :].rearrange("p (o j) -> p o j", j=PACK),
                scalar=BOX_GAIN,
                in1=spread[:, :, h * PACK : (h + 1) * PACK],
                op0=ALU.mult, op1=ALU.mult,
            )

        def neg_dp(c, sq, grouped, lo, hi):
            n, h = divmod(c, HALVES)
            first = max(lo, BOX)
            run = slice(PACK * first, PACK * hi)
            nc.vector.scalar_tensor_tensor(
                out=grouped[:, run].rearrange("p (o j) -> p o j", j=PACK),
                in0=sq[:, h, run].rearrange("p (o j) -> p o j", j=PACK),
                scalar=0.25,
                in1=g_sb[n][:, h, :, :].rearrange("p j o -> p o j")[:, first:hi, :],
                op0=ALU.subtract, op1=ALU.mult,
            )

        def quantise_and_multiply(c, grouped, codes, scales, lo, hi):
            nc.vector.quantize_mx(
                out=codes[:, lo:hi].bitcast(E5M2_X4),
                scales=scales[:, lo:hi],
                in_=grouped[:, lo * PACK : hi * PACK],
            )
            n, h = divmod(c, HALVES)
            x_codes, x_scales = x_q[n]
            k_cols = slice(h * C0, (h + 1) * C0)
            for m in range(lo // P, hi // P):
                o_cols = slice(m * P, (m + 1) * P)
                nc.tensor.matmul_mx(
                    out=acc[m][:],
                    lhsT=codes[:, o_cols].bitcast(E5M2_X4),
                    lhsT_scale=scales[:, o_cols],
                    rhs=x_codes[:, k_cols].bitcast(E4M3_X4),
                    rhs_scale=x_scales[:, k_cols],
                    start=(c == 0),
                    stop=(c == PASSES - 1),
                )

        banks = transpose_image(0)
        x_q = {}
        waiting = None
        for c in range(PASSES):
            n, h = divmod(c, HALVES)
            last_image = n == IMAGES - 1
            if h == 0:
                sq = work.tile([P, HALVES, NO * PACK], F32, name="sq")
                y_box = work.tile([P, HALVES, BOX, PACK], F32, name="y_box")
                grouped_of = []
            sigmoid_and_square(c, sq, y_box)
            if h == 0:
                x_grouped = x_work.tile([P, HALVES * C0 * PACK], BF16, name="xg", align_bytes=64)
                share = scalar_banks(n)
                copy_banks(banks, x_grouped, range(share), nc.scalar.copy)
                if n == 0:
                    copy_banks(banks, x_grouped, range(share, IMAGE_BANKS), nc.vector.tensor_copy)
            elif n + 1 < IMAGES:
                banks = transpose_image(n + 1)
            grouped = dp_work.tile([P, NO * PACK], BF16, name="dpg", align_bytes=64)
            codes = dp_work.tile([P, NO], U32, name="dc", align_bytes=64)
            scales = dp_work.tile([P, NO], U8, name="ds", align_bytes=64)
            grouped_of.append(grouped)
            if c == PASSES - 1:
                quantise_and_multiply(*waiting)
                waiting = None
            box = slice(h, h + 1) if last_image else slice(0, HALVES) if h == 1 else None
            for lo, hi in pieces_of(c):
                if lo == 0 and box is not None:
                    factors = box_factors(n, box, sq, y_box)
                neg_dp(c, sq, grouped, lo, hi)
                if lo == 0 and box is not None:
                    for done in range(box.start, box.stop):
                        box_neg_dp(done, factors, grouped_of[done])
                if h == 0 and n > 0:
                    copy_banks(banks, x_grouped, range(share, IMAGE_BANKS), nc.vector.tensor_copy)
                if waiting is not None:
                    quantise_and_multiply(*waiting)
                if h == 0 and lo == 0:
                    x_q[n] = quantise_image(x_grouped)
                waiting = (c, grouped, codes, scales, lo, hi)
        quantise_and_multiply(*waiting)

        for m in range(NO // P):
            result = results.tile([P, C0], F32, name="result")
            by_channel = acc[m][:].rearrange("p (r q) -> p q r", r=ROWS)
            width = C0 // 2 if m == NO // P - 1 else C0
            for k0 in range(0, C0, width):
                cols = slice(k0, k0 + width)
                nc.scalar.mul(
                    out=result[:, cols].rearrange("p (q r) -> p q r", r=ROWS),
                    in_=by_channel[:, k0 // ROWS : (k0 + width) // ROWS, :],
                    mul=-1.0,
                )
                nc.sync.dma_start(out=out[m * P : (m + 1) * P, cols], in_=result[:, cols])
